import numpy as np
import ml_dtypes


def mxq(x, axis, fmt="e4m3"):
    dtype, down = {"e4m3": (ml_dtypes.float8_e4m3fn, 7), "e5m2": (ml_dtypes.float8_e5m2, 14)}[fmt]
    v = np.moveaxis(np.asarray(x, np.float32).astype(ml_dtypes.bfloat16).astype(np.float64), axis, -1)
    blocks = v.reshape(v.shape[:-1] + (-1, 32))
    amax = np.abs(blocks).max(-1, keepdims=True)
    byte = np.maximum(np.where(amax > 0, np.frexp(amax)[1] - 1 + 127, 0) - down, 1)
    scale = np.exp2(byte - 127.0)
    codes = (blocks / scale).astype(np.float32).astype(dtype).astype(np.float64)
    return np.moveaxis((codes * scale).reshape(v.shape), -1, axis)


WIDE = False


def mx_kscale(k):
    if not WIDE:
        return np.ones(k)
    levels = np.array([10, -10, 5, -5, 0])
    if k % 512:
        return np.exp2(np.random.permutation(np.resize(levels, k // 32))).repeat(32)
    a = np.empty((k // 512, 16))
    for p in range(k // 512):
        a[p, :8] = np.random.permutation(np.resize(levels, 8))
        for g in range(8):
            far = levels[np.abs(levels - a[p, g]) >= 10]
            a[p, g + 8] = far[np.random.randint(len(far))]
    return np.exp2(a.ravel()).repeat(32)


BF16 = ml_dtypes.bfloat16


def bf(x):
    return np.asarray(x, np.float32).astype(BF16)


def f64(x):
    return np.asarray(x).astype(np.float64)


B, N, D, C, H, NS = 2, 1024, 1024, 1024, 16, 10
HD = C // H
D4 = (0.4829629131445341, 0.8365163037378079, 0.2241438680420134, -0.1294095225512604)


def causal_multiscale(x_c, scale_gain):
    g = np.exp(scale_gain - scale_gain.max(0, keepdims=True))
    gains = g / g.sum(0, keepdims=True)
    gains_exp = np.repeat(gains, HD, axis=1)
    out = np.zeros_like(x_c)
    for j in range(NS):
        d = 2 ** j
        xp = np.pad(x_c, ((0, 0), (0, 0), (3 * d, 0)))
        y = (D4[0] * xp[:, :, 0 * d:0 * d + N]
             + D4[1] * xp[:, :, 1 * d:1 * d + N]
             + D4[2] * xp[:, :, 2 * d:2 * d + N]
             + D4[3] * xp[:, :, 3 * d:3 * d + N])
        out = out + gains_exp[j][None, :, None] * y
    return out


def setup_inputs():
    s = mx_kscale(D)
    return {"x": bf(np.random.standard_normal((B, N, D)) * s),
            "k_w": bf(np.random.standard_normal((C, D)) / np.sqrt(D) / s[None, :]),
            "k_b": bf(np.random.standard_normal(C) * 0.2),
            "v_w": bf(np.random.standard_normal((C, D)) / np.sqrt(D) / s[None, :]),
            "v_b": bf(np.random.standard_normal(C) * 0.2),
            "scale_gain": bf(np.random.standard_normal((NS, H)) * 0.5)}


def reference(x, k_w, k_b, v_w, v_b, scale_gain):
    xq = mxq(f64(x), 2, "e4m3")
    k = ((xq @ mxq(f64(k_w), 1, "e4m3").T) + f64(k_b)).reshape(B, N, H, HD)
    v = ((xq @ mxq(f64(v_w), 1, "e4m3").T) + f64(v_b)).reshape(B, N, H, HD)
    k_mag = np.sqrt((k * k).sum(-1, keepdims=True))
    field = v * k_mag
    x_c = field.transpose(0, 2, 3, 1).reshape(B, C, N)
    return causal_multiscale(x_c, f64(scale_gain))

@@ -1,0 +1,386 @@
+from contextlib import ExitStack
+
+import concourse.mybir as mybir
+from concourse.masks import make_identity
+
+F32 = mybir.dt.float32
+BF16 = mybir.dt.bfloat16
+U32 = mybir.dt.uint32
+U8 = mybir.dt.uint8
+FP8X4 = mybir.dt.float8_e4m3fn_x4
+ALU = mybir.AluOpType
+ACT = mybir.ActivationFunctionType
+AX = mybir.AxisListType
+
+P = 128
+B, N, D, C, H, NS = 2, 1024, 1024, 1024, 16, 10
+HD = C // H
+HALF = N // 2
+T0, T1, T2, T3 = (0.4829629131445341, 0.8365163037378079, 0.2241438680420134, -0.1294095225512604)
+
+PAIRS = H // 2
+UNITS = 8 * PAIRS
+AHEAD = 12
+EARLY_PAIRS = 3
+RAW_BUFS = 6
+ROW = 320
+GROUP = 4 * ROW
+PAD = 8
+SHIFTS = ((2, 0, 1), (3, 1, 0), (6, 1, 1))
+
+FLOPS = 2 * (B * N) * D * (2 * C)
+
+
+def tile_causalwaveletfieldattentionbyte_pa_kernel(tc, x, k_w, k_b, v_w, v_b, scale_gain, out):
+    nc = tc.nc
+    with ExitStack() as ctx:
+        const = ctx.enter_context(tc.tile_pool(name="const", bufs=1))
+        rawp = ctx.enter_context(tc.tile_pool(name="rawp", bufs=RAW_BUFS))
+        grpp = ctx.enter_context(tc.tile_pool(name="grpp", bufs=4))
+        work = ctx.enter_context(tc.tile_pool(name="work", bufs=4))
+        small = ctx.enter_context(tc.tile_pool(name="small", bufs=6))
+        accp = ctx.enter_context(tc.tile_pool(name="accp", bufs=4))
+        psum = ctx.enter_context(tc.psum_pool(name="psum", bufs=1))
+        ctx.enter_context(tc.manual_schedule())
+
+        def bank(i):
+            return psum.tile([P, 512], F32, tag="b%d" % i, name="bank%d" % i)
+
+        ident = const.tile([P, P], F32)
+        make_identity(nc, ident[:])
+
+        sg_bf = const.tile([P, NS * H], BF16)
+        nc.scalar.dma_start(out=sg_bf[:], in_=scale_gain.rearrange("j h -> (j h)").partition_broadcast(P))
+        biases = grpp.tile([P, 2 * C], BF16, tag="grp", align_bytes=64)
+        nc.scalar.dma_start(out=biases[:, 0:C], in_=k_b.partition_broadcast(P))
+        nc.scalar.dma_start(out=biases[:, C:2 * C], in_=v_b.partition_broadcast(P))
+        pair_bias = const.tile([P, 2 * C], BF16)
+
+        g = const.tile([P, NS, H], F32)
+        gmax = const.tile([P, H], F32)
+        gsum = const.tile([P, H], F32)
+        grec = const.tile([P, H], F32)
+        gone = const.tile([P, H], F32)
+        pow2 = const.tile([P, NS, H], F32)
+        thr2 = const.tile([P, NS, H], F32)
+        tables = (pow2, thr2)
+        toep = const.tile([P, H * ROW], F32)
+        scratch = out[1].rearrange("c n -> (c n)")
+
+        def gains():
+            by_head = g[:].rearrange("p j h -> p h j")
+            rows = toep[:].rearrange("p (h w) -> p h w", w=ROW)
+            nc.vector.memset(toep[:], 0.0)
+            nc.vector.tensor_copy(out=g[:], in_=sg_bf[:].rearrange("p (j h) -> p j h", j=NS))
+            nc.vector.tensor_reduce(out=gmax[:], in_=by_head, axis=AX.X, op=ALU.max)
+            nc.vector.tensor_tensor(out=g[:], in0=g[:], in1=gmax[:].unsqueeze(1).to_broadcast([P, NS, H]), op=ALU.subtract)
+            nc.scalar.activation(out=g[:], in_=g[:], func=ACT.Exp)
+            nc.vector.tensor_reduce(out=gsum[:], in_=by_head, axis=AX.X, op=ALU.add)
+            nc.vector.reciprocal(out=grec[:], in_=gsum[:])
+            nc.vector.tensor_tensor(out=g[:], in0=g[:], in1=grec[:].unsqueeze(1).to_broadcast([P, NS, H]), op=ALU.mult)
+            nc.vector.tensor_scalar_mul(out=pow2[:], in0=g[:], scalar1=T2)
+            nc.vector.scalar_tensor_tensor(
+                out=pow2[:, 1:NS, :], in0=g[:, 0:NS - 1, :], scalar=T1, in1=pow2[:, 1:NS, :], op0=ALU.mult, op1=ALU.add
+            )
+            nc.vector.tensor_scalar_mul(out=thr2[:], in0=g[:], scalar1=T0)
+            nc.vector.tensor_reduce(out=gone[:], in_=by_head, axis=AX.X, op=ALU.add)
+            nc.vector.tensor_scalar_mul(out=rows[:, :, 0:1], in0=gone[:].unsqueeze(2), scalar1=T3)
+            for j in range(2, NS):
+                col = 2 ** (j - 2)
+                nc.vector.tensor_copy(out=rows[:, :, col:col + 1], in_=pow2[:, j, :].unsqueeze(2))
+            for j in range(2, NS - 1):
+                col = 3 * 2 ** (j - 2)
+                nc.vector.tensor_copy(out=rows[:, :, col:col + 1], in_=thr2[:, j, :].unsqueeze(2))
+
+        def sort_biases():
+            nc.vector.tensor_copy(
+                out=pair_bias[:].rearrange("p (r m c) -> p m r c", m=2, c=P),
+                in_=biases[:].rearrange("p (m r c) -> p m r c", m=2, c=P),
+            )
+
+        def rows_out(queue, g0, g1):
+            queue.dma_start(
+                out=scratch[g0 * P * GROUP:g1 * P * GROUP].rearrange("(g a w) -> a g w", a=P, w=GROUP),
+                in_=toep[:, g0 * GROUP:g1 * GROUP].rearrange("p (g w) -> p g w", w=GROUP),
+            )
+
+        def blocks_back(queue, gi):
+            used = 3 * ROW + 2 * P
+            skewed = scratch[gi * P * GROUP:gi * P * GROUP + P * (GROUP - 1)].rearrange("(a w) -> a w", w=GROUP - 1)
+            queue.dma_start(out=toep[:, gi * GROUP:gi * GROUP + used], in_=skewed[:, 0:used])
+
+        xq = const.tile([P, 2 * B * N], U32, align_bytes=64)
+        xs = const.tile([P, 2 * B * N], U8, align_bytes=64)
+        wq = const.tile([P, 2 * 2 * C], U32, align_bytes=64)
+        ws = const.tile([P, 2 * 2 * C], U8, align_bytes=64)
+        xq_v = xq[:].rearrange("p (g c) -> p g c", g=2)
+        xs_v = xs[:].rearrange("p (g c) -> p g c", g=2)
+        wq_v = wq[:].rearrange("p (g c) -> p g c", g=2)
+        ws_v = ws[:].rearrange("p (g c) -> p g c", g=2)
+
+        field = const.tile([P, 8 * H * 2 * HD], F32)
+        field_v = field[:].rearrange("p (q h b c) -> p q h b c", q=8, h=H, b=2)
+
+        raw, flipped, grouped = {}, {}, {}
+
+        def load_slab(slab):
+            kind, i = slab
+            raw[slab] = rawp.tile([P, 2 * D], BF16, tag="raw", name="raw")
+            halves = raw[slab][:].rearrange("p (r d) -> p r d", r=2)
+            if kind == "x":
+                tokens = x[i // 4, ((i // 2) % 2) * HALF:((i // 2) % 2 + 1) * HALF, :].rearrange("(a r) d -> a r d", r=4)
+                nc.sync.dma_start(out=halves, in_=tokens[:, 2 * (i % 2):2 * (i % 2) + 2, :])
+            else:
+                nc.sync.dma_start(out=halves[:, 0, :], in_=k_w[i * P:(i + 1) * P, :])
+                nc.sync.dma_start(out=halves[:, 1, :], in_=v_w[i * P:(i + 1) * P, :])
+
+        def flip(slab, j, bk):
+            words = raw[slab][:].bitcast(F32)
+            flipped[slab, j] = bank(bk)
+            for gu in range(4):
+                nc.tensor.transpose(
+                    flipped[slab, j][:, gu * P:(gu + 1) * P],
+                    words[:, j * 512 + (gu // 2) * 256 + gu % 2:j * 512 + (gu // 2) * 256 + 256:2],
+                    ident[:],
+                )
+
+        def regroup(slab, j):
+            if j == 0:
+                grouped[slab] = grpp.tile([P, 2 * C], BF16, tag="grp", align_bytes=64, name="grp")
+            dst = grouped[slab][:].bitcast(F32).rearrange("p (g c u) -> p g c u", g=2, u=2)[:, :, j * P:(j + 1) * P, :]
+            nc.scalar.copy(out=dst, in_=flipped[slab, j][:].rearrange("p (g u c) -> p g c u", g=2, u=2))
+
+        def quantise(slab):
+            kind, i = slab
+            codes, scales = (xq_v, xs_v) if kind == "x" else (wq_v, ws_v)
+            for gg in range(2):
+                nc.vector.quantize_mx(
+                    out=codes[:, gg, i * 256:(i + 1) * 256].bitcast(FP8X4),
+                    scales=scales[:, gg, i * 256:(i + 1) * 256],
+                    in_=grouped[slab][:, gg * C:(gg + 1) * C],
+                )
+
+        sums, biased, squares, norms = {}, {}, {}, {}
+
+        def project(u, bk):
+            if not 0 <= u < UNITS:
+                return
+            pr = u // 8
+            sums[u] = bank(bk)
+            for ti in range(2):
+                t = 2 * (u % 8) + ti
+                for gg in range(2):
+                    nc.tensor.matmul_mx(
+                        out=sums[u][:, ti * 256:(ti + 1) * 256],
+                        lhsT=xq_v[:, gg, t * P:(t + 1) * P].bitcast(FP8X4),
+                        lhsT_scale=xs_v[:, gg, t * P:(t + 1) * P],
+                        rhs=wq_v[:, gg, pr * 256:(pr + 1) * 256].bitcast(FP8X4),
+                        rhs_scale=ws_v[:, gg, pr * 256:(pr + 1) * 256],
+                        start=(gg == 0),
+                        stop=(gg == 1),
+                    )
+
+        def add_bias(u):
+            if not 0 <= u < UNITS:
+                return
+            pr = u // 8
+            biased[u] = work.tile([P, 512], F32, tag="kv", name="kv")
+            nc.vector.tensor_tensor(
+                out=biased[u][:].rearrange("p (t c) -> p t c", t=2),
+                in0=sums[u][:].rearrange("p (t c) -> p t c", t=2),
+                in1=pair_bias[:, pr * 256:(pr + 1) * 256].unsqueeze(1).to_broadcast([P, 2, 256]),
+                op=ALU.add,
+            )
+
+        def square(u):
+            if not 0 <= u < UNITS:
+                return
+            squares[u] = small.tile([P, 4], F32, tag="msq", name="msq")
+            for th in range(4):
+                lo = (th // 2) * 256 + (th % 2) * HD
+                nc.scalar.activation(
+                    out=biased[u][:, lo:lo + HD], in_=biased[u][:, lo:lo + HD], func=ACT.Square,
+                    accum_out=squares[u][:, th:th + 1],
+                )
+
+        def root(u):
+            if not 0 <= u < UNITS:
+                return
+            norms[u] = small.tile([P, 4], F32, tag="mag", name="mag")
+            nc.scalar.activation(out=norms[u][:], in_=squares[u][:], func=ACT.Sqrt)
+
+        def make_field(u):
+            if not 0 <= u < UNITS:
+                return
+            pr, t = u // 8, 2 * (u % 8)
+            nc.gpsimd.tensor_tensor(
+                out=field_v[:, t % 8:t % 8 + 2, 2 * pr:2 * pr + 2, t // 8, :],
+                in0=biased[u][:].rearrange("p (t m h c) -> p t m h c", t=2, m=2, h=2)[:, :, 1, :, :],
+                in1=norms[u][:].rearrange("p (t h) -> p t h", t=2).unsqueeze(3).to_broadcast([P, 2, 2, HD]),
+                op=ALU.mult,
+            )
+
+        def in_order(ap):
+            return ap.rearrange("p (a r) -> p a r", r=4)
+
+        def planes(ap):
+            return ap.rearrange("p (r a) -> p a r", r=4)
+
+        def stationary(h, q):
+            return field_v[:, q, h, :, :].rearrange("p b c -> p (b c)")
+
+        copy_f, toeplitz, acc, first_tap = {}, {}, {}, {}
+
+        def open_head(h):
+            for half in range(2):
+                copy_f[h, half] = bank(2 * (h % 2) + half)
+                for r in range(4):
+                    nc.tensor.transpose(copy_f[h, half][:, r * P:(r + 1) * P], stationary(h, 4 * half + r), ident[:])
+            for half in range(2):
+                acc[h, half] = accp.tile([P, HALF + PAD], F32, tag="acc%d" % half, name="acc")
+                nc.gpsimd.memset(acc[h, half][:, HALF:HALF + PAD], 0.0)
+
+        def filter_matmul(h, i):
+            near = toep[:, h * ROW:h * ROW + P]
+            far = toep[:, h * ROW + P:h * ROW + 2 * P]
+            if i == 0 or i == 4:
+                toeplitz[h, i // 4] = bank(4 + i // 4)
+            if i < 4:
+                nc.tensor.matmul(toeplitz[h, 0][:, i * P:(i + 1) * P], lhsT=stationary(h, i), rhs=near, start=True, stop=True)
+            else:
+                r = (i - 4) // 2
+                dst = toeplitz[h, 1][:, r * P:(r + 1) * P]
+                if i % 2 == 0:
+                    nc.tensor.matmul(dst, lhsT=stationary(h, r), rhs=far, start=True, stop=False)
+                else:
+                    nc.tensor.matmul(dst, lhsT=stationary(h, 4 + r), rhs=near, start=False, stop=True)
+
+        def empty_toeplitz(h, half):
+            if 0 <= h < H:
+                nc.scalar.copy(out=in_order(acc[h, half][:, 0:HALF]), in_=planes(toeplitz[h, half][:]))
+
+        def shift_one(h, half):
+            if not 0 <= h < H:
+                return
+            if half == 0:
+                first_tap[h] = accp.tile([P, N + PAD], F32, tag="one", bufs=3, name="one")
+            lo = half * HALF + 1
+            nc.scalar.activation(
+                out=in_order(first_tap[h][:, lo:lo + HALF]), in_=planes(copy_f[h, half][:]), func=ACT.Copy,
+                scale=pow2[:, 0, h:h + 1],
+            )
+
+        def tap(h, half, which):
+            if not 0 <= h < H:
+                return
+            shift, table, j = SHIFTS[which]
+            window = in_order(acc[h, half][:, shift:shift + HALF])
+            nc.vector.scalar_tensor_tensor(
+                out=window, in0=planes(copy_f[h, half][:]), scalar=tables[table][:, j, h:h + 1], in1=window,
+                op0=ALU.mult, op1=ALU.add,
+            )
+
+        def finish(h, half):
+            if not 0 <= h < H:
+                return
+            a0, a1, one = acc[h, 0], acc[h, 1], first_tap[h]
+            if half == 0:
+                nc.gpsimd.tensor_tensor(out=a0[:, 1:HALF], in0=a0[:, 1:HALF], in1=one[:, 1:HALF], op=ALU.add)
+            else:
+                nc.gpsimd.tensor_tensor(out=a1[:, 0:PAD], in0=a1[:, 0:PAD], in1=a0[:, HALF:HALF + PAD], op=ALU.add)
+                nc.gpsimd.tensor_tensor(out=a1[:, 0:HALF], in0=a1[:, 0:HALF], in1=one[:, HALF:N], op=ALU.add)
+            for b in range(2):
+                nc.sync.dma_start(
+                    out=out[b, h * HD:(h + 1) * HD, half * HALF:(half + 1) * HALF],
+                    in_=acc[h, half][b * HD:(b + 1) * HD, 0:HALF],
+                )
+
+        slabs = [("w", 0)] + [("x", i) for i in range(8)] + [("w", pr) for pr in range(1, PAIRS)]
+        early = 8 + EARLY_PAIRS
+        for slab in slabs[0:RAW_BUFS]:
+            load_slab(slab)
+        gains()
+        rows_out(nc.gpsimd, 0, 1)
+        blocks_back(nc.gpsimd, 0)
+        turn = 0
+        for s in range(AHEAD + 4):
+            if s < early:
+                flip(slabs[s], 0, turn % 8)
+                flip(slabs[s], 1, (turn + 1) % 8)
+                turn += 2
+                if s + RAW_BUFS < len(slabs):
+                    load_slab(slabs[s + RAW_BUFS])
+            if s >= 4:
+                project(s - 4, turn % 8)
+                turn += 1
+            if 1 <= s <= early:
+                regroup(slabs[s - 1], 0)
+                regroup(slabs[s - 1], 1)
+            square(s - 6)
+            root(s - 7)
+            make_field(s - 7)
+            add_bias(s - 5)
+            if 1 <= s <= early:
+                quantise(slabs[s - 1])
+            if s == 1:
+                sort_biases()
+        add_bias(AHEAD - 1)
+        rows_out(nc.sync, 1, 4)
+        for gi in range(1, 4):
+            blocks_back(nc.sync, gi)
+
+        def late_slab(h):
+            return slabs[early + h // 2] if 0 <= h < 2 * (PAIRS - EARLY_PAIRS) else None
+
+        def late_weights_in(h):
+            if late_slab(h) is not None:
+                flip(late_slab(h), h % 2, 4)
+
+        def late_weights_out(h):
+            if late_slab(h) is not None:
+                regroup(late_slab(h), h % 2)
+
+        def late_weights_quantise(h):
+            if h % 2 == 1 and late_slab(h) is not None:
+                quantise(late_slab(h))
+
+        def slot(h, p):
+            u = AHEAD + 4 * h + p
+            if p == 0:
+                empty_toeplitz(h - 1, 1)
+                finish(h - 2, 1)
+            project(u, 6 + u % 2)
+            if u - 1 >= AHEAD:
+                add_bias(u - 1)
+            square(u - 2)
+            root(u - 3)
+            make_field(u - 3)
+            if p == 0:
+                tap(h - 1, 0, 1)
+                tap(h - 1, 1, 0)
+            elif p == 1:
+                shift_one(h, 0)
+                tap(h - 1, 0, 2)
+                late_weights_quantise(h - 1)
+            elif p == 2:
+                empty_toeplitz(h, 0)
+                finish(h - 1, 0)
+                tap(h - 1, 1, 1)
+            else:
+                late_weights_out(h)
+                tap(h - 1, 1, 2)
+                tap(h, 0, 0)
+                shift_one(h, 1)
+
+        for h in range(H + 2):
+            if h < H:
+                open_head(h)
+                for i in range(12):
+                    filter_matmul(h, i)
+                    if i == 9:
+                        late_weights_in(h)
+                    if i % 3 == 1:
+                        slot(h, i // 3)
+            else:
+                for p in range(4):
+                    slot(h, p)

@@ -20,9 +20,11 @@ T0, T1, T2, T3 = (0.4829629131445341, 0.8365163037378079, 0.2241438680420134, -0
 
 PAIRS = H // 2
 UNITS = 8 * PAIRS
-AHEAD = 12
-EARLY_PAIRS = 3
-RAW_BUFS = 6
+XSLABS = 8
+AHEAD = 24
+PER_HEAD = 3
+EARLY_PAIRS = 4
+RAW_BUFS = 10
 ROW = 320
 GROUP = 4 * ROW
 PAD = 8
@@ -37,9 +39,9 @@ def tile_causalwaveletfieldattentionbyte_pa_kernel(tc, x, k_w, k_b, v_w, v_b, sc
         const = ctx.enter_context(tc.tile_pool(name="const", bufs=1))
         rawp = ctx.enter_context(tc.tile_pool(name="rawp", bufs=RAW_BUFS))
         grpp = ctx.enter_context(tc.tile_pool(name="grpp", bufs=4))
-        work = ctx.enter_context(tc.tile_pool(name="work", bufs=4))
-        small = ctx.enter_context(tc.tile_pool(name="small", bufs=6))
-        accp = ctx.enter_context(tc.tile_pool(name="accp", bufs=4))
+        work = ctx.enter_context(tc.tile_pool(name="work", bufs=6))
+        small = ctx.enter_context(tc.tile_pool(name="small", bufs=8))
+        accp = ctx.enter_context(tc.tile_pool(name="accp", bufs=3))
         psum = ctx.enter_context(tc.psum_pool(name="psum", bufs=1))
         ctx.enter_context(tc.manual_schedule())
 
@@ -51,10 +53,7 @@ def tile_causalwaveletfieldattentionbyte_pa_kernel(tc, x, k_w, k_b, v_w, v_b, sc
 
         sg_bf = const.tile([P, NS * H], BF16)
         nc.scalar.dma_start(out=sg_bf[:], in_=scale_gain.rearrange("j h -> (j h)").partition_broadcast(P))
-        biases = grpp.tile([P, 2 * C], BF16, tag="grp", align_bytes=64)
-        nc.scalar.dma_start(out=biases[:, 0:C], in_=k_b.partition_broadcast(P))
-        nc.scalar.dma_start(out=biases[:, C:2 * C], in_=v_b.partition_broadcast(P))
-        pair_bias = const.tile([P, 2 * C], BF16)
+        biases = const.tile([P, 2 * C], BF16)
 
         g = const.tile([P, NS, H], F32)
         gmax = const.tile([P, H], F32)
@@ -66,15 +65,21 @@ def tile_causalwaveletfieldattentionbyte_pa_kernel(tc, x, k_w, k_b, v_w, v_b, sc
         tables = (pow2, thr2)
         toep = const.tile([P, H * ROW], F32)
         scratch = out[1].rearrange("c n -> (c n)")
+        by_head = g[:].rearrange("p j h -> p h j")
 
-        def gains():
-            by_head = g[:].rearrange("p j h -> p h j")
-            rows = toep[:].rearrange("p (h w) -> p h w", w=ROW)
-            nc.vector.memset(toep[:], 0.0)
+        def load_biases():
+            nc.sync.dma_start(out=biases[:, 0:C], in_=k_b.partition_broadcast(P))
+            nc.sync.dma_start(out=biases[:, C:2 * C], in_=v_b.partition_broadcast(P))
+
+        def gains_exp():
+            nc.gpsimd.memset(toep[:], 0.0)
             nc.vector.tensor_copy(out=g[:], in_=sg_bf[:].rearrange("p (j h) -> p j h", j=NS))
             nc.vector.tensor_reduce(out=gmax[:], in_=by_head, axis=AX.X, op=ALU.max)
             nc.vector.tensor_tensor(out=g[:], in0=g[:], in1=gmax[:].unsqueeze(1).to_broadcast([P, NS, H]), op=ALU.subtract)
             nc.scalar.activation(out=g[:], in_=g[:], func=ACT.Exp)
+
+        def gains_rows():
+            rows = toep[:].rearrange("p (h w) -> p h w", w=ROW)
             nc.vector.tensor_reduce(out=gsum[:], in_=by_head, axis=AX.X, op=ALU.add)
             nc.vector.reciprocal(out=grec[:], in_=gsum[:])
             nc.vector.tensor_tensor(out=g[:], in0=g[:], in1=grec[:].unsqueeze(1).to_broadcast([P, NS, H]), op=ALU.mult)
@@ -91,12 +96,6 @@ def tile_causalwaveletfieldattentionbyte_pa_kernel(tc, x, k_w, k_b, v_w, v_b, sc
             for j in range(2, NS - 1):
                 col = 3 * 2 ** (j - 2)
                 nc.vector.tensor_copy(out=rows[:, :, col:col + 1], in_=thr2[:, j, :].unsqueeze(2))
-
-        def sort_biases():
-            nc.vector.tensor_copy(
-                out=pair_bias[:].rearrange("p (r m c) -> p m r c", m=2, c=P),
-                in_=biases[:].rearrange("p (m r c) -> p m r c", m=2, c=P),
-            )
 
         def rows_out(queue, g0, g1):
             queue.dma_start(
@@ -137,12 +136,12 @@ def tile_causalwaveletfieldattentionbyte_pa_kernel(tc, x, k_w, k_b, v_w, v_b, sc
         def flip(slab, j, bk):
             words = raw[slab][:].bitcast(F32)
             flipped[slab, j] = bank(bk)
-            for gu in range(4):
-                nc.tensor.transpose(
-                    flipped[slab, j][:, gu * P:(gu + 1) * P],
-                    words[:, j * 512 + (gu // 2) * 256 + gu % 2:j * 512 + (gu // 2) * 256 + 256:2],
-                    ident[:],
-                )
+            for gg in range(2):
+                for u in range(2):
+                    lo = j * 512 + gg * 256
+                    nc.tensor.transpose(
+                        flipped[slab, j][:, (2 * gg + u) * P:(2 * gg + u + 1) * P], words[:, lo + u:lo + 256:2], ident[:]
+                    )
 
         def regroup(slab, j):
             if j == 0:
@@ -163,8 +162,6 @@ def tile_causalwaveletfieldattentionbyte_pa_kernel(tc, x, k_w, k_b, v_w, v_b, sc
         sums, biased, squares, norms = {}, {}, {}, {}
 
         def project(u, bk):
-            if not 0 <= u < UNITS:
-                return
             pr = u // 8
             sums[u] = bank(bk)
             for ti in range(2):
@@ -181,20 +178,17 @@ def tile_causalwaveletfieldattentionbyte_pa_kernel(tc, x, k_w, k_b, v_w, v_b, sc
                     )
 
         def add_bias(u):
-            if not 0 <= u < UNITS:
-                return
             pr = u // 8
             biased[u] = work.tile([P, 512], F32, tag="kv", name="kv")
+            pair = biases[:].rearrange("p (m c) -> p m c", m=2)[:, :, pr * P:(pr + 1) * P]
             nc.vector.tensor_tensor(
-                out=biased[u][:].rearrange("p (t c) -> p t c", t=2),
-                in0=sums[u][:].rearrange("p (t c) -> p t c", t=2),
-                in1=pair_bias[:, pr * 256:(pr + 1) * 256].unsqueeze(1).to_broadcast([P, 2, 256]),
+                out=biased[u][:].rearrange("p (t m c) -> p t m c", t=2, m=2),
+                in0=sums[u][:].rearrange("p (t m c) -> p t m c", t=2, m=2),
+                in1=pair.unsqueeze(1).to_broadcast([P, 2, 2, P]),
                 op=ALU.add,
             )
 
         def square(u):
-            if not 0 <= u < UNITS:
-                return
             squares[u] = small.tile([P, 4], F32, tag="msq", name="msq")
             for th in range(4):
                 lo = (th // 2) * 256 + (th % 2) * HD
@@ -204,14 +198,10 @@ def tile_causalwaveletfieldattentionbyte_pa_kernel(tc, x, k_w, k_b, v_w, v_b, sc
                 )
 
         def root(u):
-            if not 0 <= u < UNITS:
-                return
             norms[u] = small.tile([P, 4], F32, tag="mag", name="mag")
             nc.scalar.activation(out=norms[u][:], in_=squares[u][:], func=ACT.Sqrt)
 
         def make_field(u):
-            if not 0 <= u < UNITS:
-                return
             pr, t = u // 8, 2 * (u % 8)
             nc.gpsimd.tensor_tensor(
                 out=field_v[:, t % 8:t % 8 + 2, 2 * pr:2 * pr + 2, t // 8, :],
@@ -229,16 +219,15 @@ def tile_causalwaveletfieldattentionbyte_pa_kernel(tc, x, k_w, k_b, v_w, v_b, sc
         def stationary(h, q):
             return field_v[:, q, h, :, :].rearrange("p b c -> p (b c)")
 
-        copy_f, toeplitz, acc, first_tap = {}, {}, {}, {}
+        copy_f, toeplitz, result, taps = {}, {}, {}, {}
 
         def open_head(h):
             for half in range(2):
                 copy_f[h, half] = bank(2 * (h % 2) + half)
                 for r in range(4):
                     nc.tensor.transpose(copy_f[h, half][:, r * P:(r + 1) * P], stationary(h, 4 * half + r), ident[:])
-            for half in range(2):
-                acc[h, half] = accp.tile([P, HALF + PAD], F32, tag="acc%d" % half, name="acc")
-                nc.gpsimd.memset(acc[h, half][:, HALF:HALF + PAD], 0.0)
+            taps[h] = accp.tile([P, N + PAD], F32, tag="taps", name="taps")
+            nc.gpsimd.memset(taps[h][:, N + 1:N + PAD], 0.0)
 
         def filter_matmul(h, i):
             near = toep[:, h * ROW:h * ROW + P]
@@ -256,131 +245,160 @@ def tile_causalwaveletfieldattentionbyte_pa_kernel(tc, x, k_w, k_b, v_w, v_b, sc
                     nc.tensor.matmul(dst, lhsT=stationary(h, 4 + r), rhs=near, start=False, stop=True)
 
         def empty_toeplitz(h, half):
-            if 0 <= h < H:
-                nc.scalar.copy(out=in_order(acc[h, half][:, 0:HALF]), in_=planes(toeplitz[h, half][:]))
+            result[h, half] = accp.tile([P, HALF], F32, tag="res%d" % half, name="res")
+            nc.scalar.copy(out=in_order(result[h, half][:]), in_=planes(toeplitz[h, half][:]))
 
         def shift_one(h, half):
-            if not 0 <= h < H:
-                return
-            if half == 0:
-                first_tap[h] = accp.tile([P, N + PAD], F32, tag="one", bufs=3, name="one")
             lo = half * HALF + 1
             nc.scalar.activation(
-                out=in_order(first_tap[h][:, lo:lo + HALF]), in_=planes(copy_f[h, half][:]), func=ACT.Copy,
+                out=in_order(taps[h][:, lo:lo + HALF]), in_=planes(copy_f[h, half][:]), func=ACT.Copy,
                 scale=pow2[:, 0, h:h + 1],
             )
 
         def tap(h, half, which):
-            if not 0 <= h < H:
-                return
             shift, table, j = SHIFTS[which]
-            window = in_order(acc[h, half][:, shift:shift + HALF])
+            window = in_order(taps[h][:, half * HALF + shift:half * HALF + shift + HALF])
             nc.vector.scalar_tensor_tensor(
                 out=window, in0=planes(copy_f[h, half][:]), scalar=tables[table][:, j, h:h + 1], in1=window,
                 op0=ALU.mult, op1=ALU.add,
             )
 
-        def finish(h, half):
-            if not 0 <= h < H:
-                return
-            a0, a1, one = acc[h, 0], acc[h, 1], first_tap[h]
-            if half == 0:
-                nc.gpsimd.tensor_tensor(out=a0[:, 1:HALF], in0=a0[:, 1:HALF], in1=one[:, 1:HALF], op=ALU.add)
-            else:
-                nc.gpsimd.tensor_tensor(out=a1[:, 0:PAD], in0=a1[:, 0:PAD], in1=a0[:, HALF:HALF + PAD], op=ALU.add)
-                nc.gpsimd.tensor_tensor(out=a1[:, 0:HALF], in0=a1[:, 0:HALF], in1=one[:, HALF:N], op=ALU.add)
+        def store(h, half):
             for b in range(2):
                 nc.sync.dma_start(
                     out=out[b, h * HD:(h + 1) * HD, half * HALF:(half + 1) * HALF],
-                    in_=acc[h, half][b * HD:(b + 1) * HD, 0:HALF],
+                    in_=result[h, half][b * HD:(b + 1) * HD, :],
                 )
 
-        slabs = [("w", 0)] + [("x", i) for i in range(8)] + [("w", pr) for pr in range(1, PAIRS)]
-        early = 8 + EARLY_PAIRS
-        for slab in slabs[0:RAW_BUFS]:
+        def finish(h, half):
+            lo = 1 - half
+            res = result[h, half][:, lo:HALF]
+            nc.gpsimd.tensor_tensor(out=res, in0=res, in1=taps[h][:, half * HALF + lo:(half + 1) * HALF], op=ALU.add)
+            store(h, half)
+
+        def finish_on_vector(h, half):
+            result[h, half] = accp.tile([P, HALF], F32, tag="res%d" % half, name="res")
+            nc.vector.tensor_tensor(
+                out=in_order(result[h, half][:]), in0=planes(toeplitz[h, half][:]),
+                in1=in_order(taps[h][:, half * HALF:(half + 1) * HALF]), op=ALU.add,
+            )
+            store(h, half)
+
+        slabs = [("w", 0), ("w", 1)] + [("x", i) for i in range(XSLABS)] + [("w", pr) for pr in range(2, PAIRS)]
+        late = [(("w", EARLY_PAIRS + k // 2), k % 2) for k in range(2 * (PAIRS - EARLY_PAIRS))]
+
+        made = []
+
+        def later_stages(s):
+            for back, stage in ((1, add_bias), (2, square), (3, root), (3, make_field)):
+                if 0 <= s - back < len(made):
+                    for u in made[s - back]:
+                        stage(u)
+
+        load_slab(slabs[0])
+        load_slab(slabs[1])
+        load_slab(slabs[2])
+        load_slab(slabs[3])
+        load_biases()
+        for slab in slabs[4:RAW_BUFS]:
             load_slab(slab)
-        gains()
-        rows_out(nc.gpsimd, 0, 1)
-        blocks_back(nc.gpsimd, 0)
-        turn = 0
-        for s in range(AHEAD + 4):
-            if s < early:
-                flip(slabs[s], 0, turn % 8)
-                flip(slabs[s], 1, (turn + 1) % 8)
-                turn += 2
-                if s + RAW_BUFS < len(slabs):
-                    load_slab(slabs[s + RAW_BUFS])
+        gains_exp()
+
+        early = 2 + XSLABS + EARLY_PAIRS - 2
+        for s in range(early):
+            a = 4 * (s % 2)
+            flip(slabs[s], 0, a)
+            flip(slabs[s], 1, a + 1)
+            if 1 <= s and s - 1 + RAW_BUFS < len(slabs):
+                load_slab(slabs[s - 1 + RAW_BUFS])
+            made.append([])
             if s >= 4:
-                project(s - 4, turn % 8)
-                turn += 1
-            if 1 <= s <= early:
+                for pr in range(2):
+                    u = 8 * pr + s - 4
+                    project(u, a + 2 + pr)
+                    made[s].append(u)
+            if s >= 1:
                 regroup(slabs[s - 1], 0)
                 regroup(slabs[s - 1], 1)
-            square(s - 6)
-            root(s - 7)
-            make_field(s - 7)
-            add_bias(s - 5)
-            if 1 <= s <= early:
+            later_stages(s)
+            if s >= 1:
                 quantise(slabs[s - 1])
-            if s == 1:
-                sort_biases()
-        add_bias(AHEAD - 1)
-        rows_out(nc.sync, 1, 4)
-        for gi in range(1, 4):
-            blocks_back(nc.sync, gi)
+            if s == 3:
+                gains_rows()
+                rows_out(nc.sync, 0, 1)
+                rows_out(nc.sync, 1, 4)
+                for gi in range(4):
+                    blocks_back(nc.sync, gi)
 
-        def late_slab(h):
-            return slabs[early + h // 2] if 0 <= h < 2 * (PAIRS - EARLY_PAIRS) else None
+        for k, banks in enumerate(((0, 1), (3, 6), (7, 4), (5, 2))):
+            s = early + k
+            if k == 0:
+                flip(late[0][0], late[0][1], 2)
+            made.append([16 + 2 * k, 17 + 2 * k])
+            for u, bk in zip(made[s], banks):
+                project(u, bk)
+            if k == 0:
+                regroup(slabs[early - 1], 0)
+                regroup(slabs[early - 1], 1)
+            if k == 1:
+                regroup(late[0][0], late[0][1])
+            later_stages(s)
+            if k == 0:
+                quantise(slabs[early - 1])
 
-        def late_weights_in(h):
-            if late_slab(h) is not None:
-                flip(late_slab(h), h % 2, 4)
+        first_slot = len(made)
 
-        def late_weights_out(h):
-            if late_slab(h) is not None:
-                regroup(late_slab(h), h % 2)
+        def base(h):
+            return 4 * h - (2 if h == H - 1 else 0)
 
-        def late_weights_quantise(h):
-            if h % 2 == 1 and late_slab(h) is not None:
-                quantise(late_slab(h))
-
-        def slot(h, p):
-            u = AHEAD + 4 * h + p
-            if p == 0:
+        def slot(i):
+            h, p = divmod(i, 4)
+            if p == 0 and 1 <= h < len(late):
+                regroup(late[h][0], late[h][1])
+            if p == 0 and 0 <= h - 1 < H - 1:
                 empty_toeplitz(h - 1, 1)
-                finish(h - 2, 1)
-            project(u, 6 + u % 2)
-            if u - 1 >= AHEAD:
-                add_bias(u - 1)
-            square(u - 2)
-            root(u - 3)
-            make_field(u - 3)
-            if p == 0:
-                tap(h - 1, 0, 1)
-                tap(h - 1, 1, 0)
-            elif p == 1:
-                shift_one(h, 0)
-                tap(h - 1, 0, 2)
-                late_weights_quantise(h - 1)
-            elif p == 2:
+            if p == 2 and h < H:
                 empty_toeplitz(h, 0)
-                finish(h - 1, 0)
-                tap(h - 1, 1, 1)
-            else:
-                late_weights_out(h)
-                tap(h - 1, 1, 2)
-                tap(h, 0, 0)
-                shift_one(h, 1)
+            made.append([])
+            u = AHEAD + PER_HEAD * h + p
+            if p < PER_HEAD and u < UNITS:
+                project(u, 6 + p % 2)
+                made[first_slot + i].append(u)
+            active = [(hh, i - base(hh)) for hh in range(H) if 0 <= i - base(hh) < 8]
+            for hh, age in active:
+                if age == 0 and hh == H - 1:
+                    open_head(hh)
+                if age < 2:
+                    shift_one(hh, age)
+            later_stages(first_slot + i)
+            for hh, age in active:
+                if age == 6:
+                    tap(hh, 1, 0)
+                    finish(hh, 0)
+                    if hh == H - 1:
+                        finish_on_vector(hh, 1)
+                if age == 7 and hh < H - 1:
+                    finish(hh, 1)
+                if age == 5:
+                    tap(hh, 0, 2)
+                if age == 2:
+                    tap(hh, 0, 0)
+                if age == 3:
+                    tap(hh, 1, 2)
+                    tap(hh, 0, 1)
+                if age == 4:
+                    tap(hh, 1, 1)
+            if p == 2 and h % 2 == 1 and h < len(late):
+                quantise(late[h][0])
 
-        for h in range(H + 2):
-            if h < H:
+        for h in range(H):
+            if h < H - 1:
                 open_head(h)
-                for i in range(12):
-                    filter_matmul(h, i)
-                    if i == 9:
-                        late_weights_in(h)
-                    if i % 3 == 1:
-                        slot(h, i // 3)
-            else:
-                for p in range(4):
-                    slot(h, p)
+            for i in range(12):
+                filter_matmul(h, i)
+                if i % 3 == 1 and i < 10:
+                    slot(4 * h + i // 3)
+            if h + 1 < len(late):
+                flip(late[h + 1][0], late[h + 1][1], 7)
+            slot(4 * h + 3)
+        slot(4 * H)

@@ -50,10 +50,19 @@ def tile_causalwaveletfieldattentionbyte_pa_kernel(tc, x, k_w, k_b, v_w, v_b, sc
 
         ident = const.tile([P, P], F32)
         make_identity(nc, ident[:])
+        ident_bf = const.tile([P, P], BF16)
+        make_identity(nc, ident_bf[:])
 
-        sg_bf = const.tile([P, NS * H], BF16)
-        nc.scalar.dma_start(out=sg_bf[:], in_=scale_gain.rearrange("j h -> (j h)").partition_broadcast(P))
         biases = const.tile([P, 2 * C], BF16)
+        small_rows = const.tile([P, P], BF16)
+        small_columns = const.tile([P, P], BF16)
+        nc.vector.memset(small_rows[:], 0.0)
+        nc.scalar.dma_start(out=small_rows[0:PAIRS, :], in_=k_b.rearrange("(m c) -> m c", c=P))
+        nc.scalar.dma_start(out=small_rows[PAIRS:2 * PAIRS, :], in_=v_b.rearrange("(m c) -> m c", c=P))
+        gain_logits = scale_gain.rearrange("j h -> (j h)")
+        for m in range(2):
+            part = gain_logits[m * P:min(NS * H, (m + 1) * P)].rearrange("(o c) -> o c", o=1)
+            nc.scalar.dma_start(out=small_rows[2 * PAIRS + m:2 * PAIRS + m + 1, 0:part.shape[1]], in_=part)
 
         g = const.tile([P, NS, H], F32)
         gmax = const.tile([P, H], F32)
@@ -67,35 +76,60 @@ def tile_causalwaveletfieldattentionbyte_pa_kernel(tc, x, k_w, k_b, v_w, v_b, sc
         scratch = out[1].rearrange("c n -> (c n)")
         by_head = g[:].rearrange("p j h -> p h j")
 
-        def load_biases():
-            nc.sync.dma_start(out=biases[:, 0:C], in_=k_b.partition_broadcast(P))
-            nc.sync.dma_start(out=biases[:, C:2 * C], in_=v_b.partition_broadcast(P))
+        nc.gpsimd.memset(toep[:], 0.0)
+        bias_banks = {}
+
+        def bank_bf(i):
+            return psum.tile([P, 1024], BF16, tag="b%d" % i, name="bank_bf%d" % i)
+
+        def turn_biases(bk):
+            bias_banks["columns"] = bank_bf(bk)
+            nc.tensor.transpose(bias_banks["columns"][:, 0:P], small_rows[:], ident_bf[:])
+
+        def spread_biases(q, bk):
+            bias_banks[q] = bank_bf(bk)
+            for m in range(4 if q else 6):
+                source = 4 * q + m if m < 4 else 2 * PAIRS + m - 4
+                column = small_columns[:, source:source + 1].to_broadcast([P, P])
+                nc.tensor.transpose(bias_banks[q][:, m * P:(m + 1) * P], column, ident_bf[:])
 
         def gains_exp():
-            nc.gpsimd.memset(toep[:], 0.0)
-            nc.vector.tensor_copy(out=g[:], in_=sg_bf[:].rearrange("p (j h) -> p j h", j=NS))
+            logits = bias_banks[0][:, 512:512 + NS * H]
+            nc.vector.tensor_copy(out=g[:], in_=logits.rearrange("p (j h) -> p j h", j=NS))
             nc.vector.tensor_reduce(out=gmax[:], in_=by_head, axis=AX.X, op=ALU.max)
             nc.vector.tensor_tensor(out=g[:], in0=g[:], in1=gmax[:].unsqueeze(1).to_broadcast([P, NS, H]), op=ALU.subtract)
             nc.scalar.activation(out=g[:], in_=g[:], func=ACT.Exp)
 
-        def gains_rows():
-            rows = toep[:].rearrange("p (h w) -> p h w", w=ROW)
-            nc.vector.tensor_reduce(out=gsum[:], in_=by_head, axis=AX.X, op=ALU.add)
-            nc.vector.reciprocal(out=grec[:], in_=gsum[:])
+        rows = toep[:].rearrange("p (h w) -> p h w", w=ROW)
+
+        def divide():
             nc.vector.tensor_tensor(out=g[:], in0=g[:], in1=grec[:].unsqueeze(1).to_broadcast([P, NS, H]), op=ALU.mult)
-            nc.vector.tensor_scalar_mul(out=pow2[:], in0=g[:], scalar1=T2)
+
+        def add_t1():
             nc.vector.scalar_tensor_tensor(
                 out=pow2[:, 1:NS, :], in0=g[:, 0:NS - 1, :], scalar=T1, in1=pow2[:, 1:NS, :], op0=ALU.mult, op1=ALU.add
             )
-            nc.vector.tensor_scalar_mul(out=thr2[:], in0=g[:], scalar1=T0)
-            nc.vector.tensor_reduce(out=gone[:], in_=by_head, axis=AX.X, op=ALU.add)
-            nc.vector.tensor_scalar_mul(out=rows[:, :, 0:1], in0=gone[:].unsqueeze(2), scalar1=T3)
-            for j in range(2, NS):
-                col = 2 ** (j - 2)
-                nc.vector.tensor_copy(out=rows[:, :, col:col + 1], in_=pow2[:, j, :].unsqueeze(2))
-            for j in range(2, NS - 1):
-                col = 3 * 2 ** (j - 2)
-                nc.vector.tensor_copy(out=rows[:, :, col:col + 1], in_=thr2[:, j, :].unsqueeze(2))
+
+        def place(col, table, j):
+            return lambda: nc.vector.tensor_copy(out=rows[:, :, col:col + 1], in_=table[:, j, :].unsqueeze(2))
+
+        gain_steps = [
+            lambda: nc.vector.tensor_reduce(out=gsum[:], in_=by_head, axis=AX.X, op=ALU.add),
+            lambda: nc.vector.reciprocal(out=grec[:], in_=gsum[:]),
+            divide,
+            lambda: nc.vector.tensor_scalar_mul(out=pow2[:], in0=g[:], scalar1=T2),
+            lambda: nc.vector.tensor_scalar_mul(out=thr2[:], in0=g[:], scalar1=T0),
+            lambda: nc.vector.tensor_reduce(out=gone[:], in_=by_head, axis=AX.X, op=ALU.add),
+            add_t1,
+            lambda: nc.vector.tensor_scalar_mul(out=rows[:, :, 0:1], in0=gone[:].unsqueeze(2), scalar1=T3),
+        ]
+        gain_steps += [place(2 ** (j - 2), pow2, j) for j in range(2, NS)]
+        gain_steps += [place(3 * 2 ** (j - 2), thr2, j) for j in range(2, NS - 1)]
+
+        def take_gain_steps(count):
+            for step in gain_steps[0:count]:
+                step()
+                gain_steps.remove(step)
 
         def rows_out(queue, g0, g1):
             queue.dma_start(
@@ -294,15 +328,15 @@ def tile_causalwaveletfieldattentionbyte_pa_kernel(tc, x, k_w, k_b, v_w, v_b, sc
                 if 0 <= s - back < len(made):
                     for u in made[s - back]:
                         stage(u)
+                        if back == 1:
+                            take_gain_steps(2)
 
         load_slab(slabs[0])
         load_slab(slabs[1])
         load_slab(slabs[2])
         load_slab(slabs[3])
-        load_biases()
         for slab in slabs[4:RAW_BUFS]:
             load_slab(slab)
-        gains_exp()
 
         early = 2 + XSLABS + EARLY_PAIRS - 2
         for s in range(early):
@@ -317,20 +351,33 @@ def tile_causalwaveletfieldattentionbyte_pa_kernel(tc, x, k_w, k_b, v_w, v_b, sc
                     u = 8 * pr + s - 4
                     project(u, a + 2 + pr)
                     made[s].append(u)
+            if s == 1:
+                turn_biases(2)
+            if s in (2, 3):
+                spread_biases(2 * s - 4, a + 2)
+                spread_biases(2 * s - 3, a + 3)
+            if s == 1:
+                nc.vector.tensor_copy(out=small_columns[:], in_=bias_banks["columns"][:, 0:P])
             if s >= 1:
                 regroup(slabs[s - 1], 0)
                 regroup(slabs[s - 1], 1)
+            if s in (3, 4):
+                for q in (2 * s - 6, 2 * s - 5):
+                    nc.vector.tensor_copy(out=biases[:, q * 512:(q + 1) * 512], in_=bias_banks[q][:, 0:512])
             later_stages(s)
             if s >= 1:
                 quantise(slabs[s - 1])
             if s == 3:
-                gains_rows()
+                gains_exp()
+            if s > 3:
+                take_gain_steps(1)
+            if s == 9:
                 rows_out(nc.sync, 0, 1)
                 rows_out(nc.sync, 1, 4)
                 for gi in range(4):
                     blocks_back(nc.sync, gi)
 
-        for k, banks in enumerate(((0, 1), (3, 6), (7, 4), (5, 2))):
+        for k, banks in enumerate(((0, 1), (6, 4), (7, 5), (3, 2))):
             s = early + k
             if k == 0:
                 flip(late[0][0], late[0][1], 2)

@@ -22,13 +22,15 @@ PAIRS = H // 2
 UNITS = 8 * PAIRS
 XSLABS = 8
 AHEAD = 24
-PER_HEAD = 3
 EARLY_PAIRS = 4
-RAW_BUFS = 10
+RAW_BUFS = 9
 ROW = 320
 GROUP = 4 * ROW
 PAD = 8
 SHIFTS = ((2, 0, 1), (3, 1, 0), (6, 1, 1))
+QUICK = 12
+TAPS_LATER = ((), (), ((0, 0),), ((1, 2), (0, 1)), ((1, 1),), ((0, 2),), ((1, 0),), ())
+TAPS_SOON = ((), ((0, 0),), ((1, 2), (0, 1)), ((1, 1),), ((0, 2), (1, 0)), (), (), ())
 
 FLOPS = 2 * (B * N) * D * (2 * C)
 
@@ -39,7 +41,8 @@ def tile_causalwaveletfieldattentionbyte_pa_kernel(tc, x, k_w, k_b, v_w, v_b, sc
         const = ctx.enter_context(tc.tile_pool(name="const", bufs=1))
         rawp = ctx.enter_context(tc.tile_pool(name="rawp", bufs=RAW_BUFS))
         grpp = ctx.enter_context(tc.tile_pool(name="grpp", bufs=4))
-        work = ctx.enter_context(tc.tile_pool(name="work", bufs=6))
+        sortp = ctx.enter_context(tc.tile_pool(name="sortp", bufs=2))
+        work = ctx.enter_context(tc.tile_pool(name="work", bufs=8))
         small = ctx.enter_context(tc.tile_pool(name="small", bufs=8))
         accp = ctx.enter_context(tc.tile_pool(name="accp", bufs=3))
         psum = ctx.enter_context(tc.psum_pool(name="psum", bufs=1))
@@ -69,6 +72,7 @@ def tile_causalwaveletfieldattentionbyte_pa_kernel(tc, x, k_w, k_b, v_w, v_b, sc
         gsum = const.tile([P, H], F32)
         grec = const.tile([P, H], F32)
         gone = const.tile([P, H], F32)
+        warm = const.tile([P, 1], F32)
         pow2 = const.tile([P, NS, H], F32)
         thr2 = const.tile([P, NS, H], F32)
         tables = (pow2, thr2)
@@ -93,12 +97,11 @@ def tile_causalwaveletfieldattentionbyte_pa_kernel(tc, x, k_w, k_b, v_w, v_b, sc
                 column = small_columns[:, source:source + 1].to_broadcast([P, P])
                 nc.tensor.transpose(bias_banks[q][:, m * P:(m + 1) * P], column, ident_bf[:])
 
-        def gains_exp():
+        def gains_top():
             logits = bias_banks[0][:, 512:512 + NS * H]
             nc.vector.tensor_copy(out=g[:], in_=logits.rearrange("p (j h) -> p j h", j=NS))
             nc.vector.tensor_reduce(out=gmax[:], in_=by_head, axis=AX.X, op=ALU.max)
             nc.vector.tensor_tensor(out=g[:], in0=g[:], in1=gmax[:].unsqueeze(1).to_broadcast([P, NS, H]), op=ALU.subtract)
-            nc.scalar.activation(out=g[:], in_=g[:], func=ACT.Exp)
 
         rows = toep[:].rearrange("p (h w) -> p h w", w=ROW)
 
@@ -154,7 +157,7 @@ def tile_causalwaveletfieldattentionbyte_pa_kernel(tc, x, k_w, k_b, v_w, v_b, sc
         field = const.tile([P, 8 * H * 2 * HD], F32)
         field_v = field[:].rearrange("p (q h b c) -> p q h b c", q=8, h=H, b=2)
 
-        raw, flipped, grouped = {}, {}, {}
+        raw, sorted_words, flipped, grouped = {}, {}, {}, {}
 
         def load_slab(slab):
             kind, i = slab
@@ -164,18 +167,29 @@ def tile_causalwaveletfieldattentionbyte_pa_kernel(tc, x, k_w, k_b, v_w, v_b, sc
                 tokens = x[i // 4, ((i // 2) % 2) * HALF:((i // 2) % 2 + 1) * HALF, :].rearrange("(a r) d -> a r d", r=4)
                 nc.sync.dma_start(out=halves, in_=tokens[:, 2 * (i % 2):2 * (i % 2) + 2, :])
             else:
-                nc.sync.dma_start(out=halves[:, 0, :], in_=k_w[i * P:(i + 1) * P, :])
+                for lo in range(0, D, D // 2 if i == 0 else D):
+                    hi = lo + (D // 2 if i == 0 else D)
+                    nc.sync.dma_start(out=halves[:, 0, lo:hi], in_=k_w[i * P:(i + 1) * P, lo:hi])
                 nc.sync.dma_start(out=halves[:, 1, :], in_=v_w[i * P:(i + 1) * P, :])
 
+        def sort_words(slab, j):
+            sorted_words[slab, j] = sortp.tile([P, D], BF16, tag="sorted", name="sorted")
+            nc.scalar.copy(
+                out=sorted_words[slab, j][:].bitcast(F32).rearrange("p (q u w) -> p q u w", u=2, w=P),
+                in_=raw[slab][:, j * D:(j + 1) * D].bitcast(F32).rearrange("p (q w u) -> p q u w", u=2, w=P),
+            )
+
         def flip(slab, j, bk):
-            words = raw[slab][:].bitcast(F32)
             flipped[slab, j] = bank(bk)
             for gg in range(2):
                 for u in range(2):
-                    lo = j * 512 + gg * 256
-                    nc.tensor.transpose(
-                        flipped[slab, j][:, (2 * gg + u) * P:(2 * gg + u + 1) * P], words[:, lo + u:lo + 256:2], ident[:]
-                    )
+                    if (slab, j) in sorted_words:
+                        lo = gg * 256 + u * P
+                        words = sorted_words[slab, j][:].bitcast(F32)[:, lo:lo + P]
+                    else:
+                        lo = j * 512 + gg * 256
+                        words = raw[slab][:].bitcast(F32)[:, lo + u:lo + 256:2]
+                    nc.tensor.transpose(flipped[slab, j][:, (2 * gg + u) * P:(2 * gg + u + 1) * P], words, ident[:])
 
         def regroup(slab, j):
             if j == 0:
@@ -368,8 +382,12 @@ def tile_causalwaveletfieldattentionbyte_pa_kernel(tc, x, k_w, k_b, v_w, v_b, sc
             if s >= 1:
                 quantise(slabs[s - 1])
             if s == 3:
-                gains_exp()
-            if s > 3:
+                gains_top()
+            if s == 4:
+                nc.scalar.activation(out=g[:], in_=g[:], func=ACT.Exp)
+            if s == 5:
+                nc.scalar.activation(out=warm[:], in_=ident[:, 0:1], func=ACT.Sqrt)
+            if s > 4:
                 take_gain_steps(1)
             if s == 9:
                 rows_out(nc.sync, 0, 1)
@@ -396,7 +414,7 @@ def tile_causalwaveletfieldattentionbyte_pa_kernel(tc, x, k_w, k_b, v_w, v_b, sc
         first_slot = len(made)
 
         def base(h):
-            return 4 * h - (2 if h == H - 1 else 0)
+            return 4 * h - max(0, h - QUICK)
 
         def slot(i):
             h, p = divmod(i, 4)
@@ -407,39 +425,34 @@ def tile_causalwaveletfieldattentionbyte_pa_kernel(tc, x, k_w, k_b, v_w, v_b, sc
             if p == 2 and h < H:
                 empty_toeplitz(h, 0)
             made.append([])
-            u = AHEAD + PER_HEAD * h + p
-            if p < PER_HEAD and u < UNITS:
+            u = AHEAD + 4 * h + p - min(h, len(late) - 1)
+            if u < UNITS and (p < 3 or h + 1 >= len(late)):
                 project(u, 6 + p % 2)
                 made[first_slot + i].append(u)
             active = [(hh, i - base(hh)) for hh in range(H) if 0 <= i - base(hh) < 8]
             for hh, age in active:
-                if age == 0 and hh == H - 1:
+                if age == 0 and hh > QUICK:
                     open_head(hh)
                 if age < 2:
                     shift_one(hh, age)
             later_stages(first_slot + i)
             for hh, age in active:
-                if age == 6:
-                    tap(hh, 1, 0)
+                schedule = TAPS_LATER if hh < QUICK else TAPS_SOON
+                for half, which in schedule[age]:
+                    tap(hh, half, which)
+                if i == (4 * hh + 6 if hh < QUICK else 4 * hh + 4):
                     finish(hh, 0)
-                    if hh == H - 1:
-                        finish_on_vector(hh, 1)
-                if age == 7 and hh < H - 1:
+                if hh == H - 1 and i == 4 * H:
+                    finish_on_vector(hh, 1)
+                if hh < H - 1 and i == (4 * hh + 7 if hh < QUICK else 4 * hh + 5):
                     finish(hh, 1)
-                if age == 5:
-                    tap(hh, 0, 2)
-                if age == 2:
-                    tap(hh, 0, 0)
-                if age == 3:
-                    tap(hh, 1, 2)
-                    tap(hh, 0, 1)
-                if age == 4:
-                    tap(hh, 1, 1)
             if p == 2 and h % 2 == 1 and h < len(late):
                 quantise(late[h][0])
+            if p == 1 and h + 1 < len(late):
+                sort_words(late[h + 1][0], late[h + 1][1])
 
         for h in range(H):
-            if h < H - 1:
+            if h <= QUICK:
                 open_head(h)
             for i in range(12):
                 filter_matmul(h, i)

@@ -145,14 +145,11 @@ def tile_causalwaveletfieldattentionbyte_pa_kernel(tc, x, k_w, k_b, v_w, v_b, sc
             skewed = scratch[gi * P * GROUP:gi * P * GROUP + P * (GROUP - 1)].rearrange("(a w) -> a w", w=GROUP - 1)
             queue.dma_start(out=toep[:, gi * GROUP:gi * GROUP + used], in_=skewed[:, 0:used])
 
-        xq = const.tile([P, 2 * B * N], U32, align_bytes=64)
-        xs = const.tile([P, 2 * B * N], U8, align_bytes=64)
-        wq = const.tile([P, 2 * 2 * C], U32, align_bytes=64)
-        ws = const.tile([P, 2 * 2 * C], U8, align_bytes=64)
-        xq_v = xq[:].rearrange("p (g c) -> p g c", g=2)
-        xs_v = xs[:].rearrange("p (g c) -> p g c", g=2)
-        wq_v = wq[:].rearrange("p (g c) -> p g c", g=2)
-        ws_v = ws[:].rearrange("p (g c) -> p g c", g=2)
+        xq = const.tile([P, 2 * B * N], U32, align_bytes=256)
+        xs = const.tile([P, 2 * B * N], U8, align_bytes=256)
+        wq = const.tile([P, 2 * 2 * C], U32, align_bytes=256)
+        ws = const.tile([P, 2 * 2 * C], U8, align_bytes=256)
+        SLAB = 512
 
         field = const.tile([P, 8 * H * 2 * HD], F32)
         field_v = field[:].rearrange("p (q h b c) -> p q h b c", q=8, h=H, b=2)
@@ -199,13 +196,11 @@ def tile_causalwaveletfieldattentionbyte_pa_kernel(tc, x, k_w, k_b, v_w, v_b, sc
 
         def quantise(slab):
             kind, i = slab
-            codes, scales = (xq_v, xs_v) if kind == "x" else (wq_v, ws_v)
-            for gg in range(2):
-                nc.vector.quantize_mx(
-                    out=codes[:, gg, i * 256:(i + 1) * 256].bitcast(FP8X4),
-                    scales=scales[:, gg, i * 256:(i + 1) * 256],
-                    in_=grouped[slab][:, gg * C:(gg + 1) * C],
-                )
+            codes, scales = (xq, xs) if kind == "x" else (wq, ws)
+            nc.vector.quantize_mx(
+                out=codes[:, i * SLAB:(i + 1) * SLAB].bitcast(FP8X4), scales=scales[:, i * SLAB:(i + 1) * SLAB],
+                in_=grouped[slab][:],
+            )
 
         sums, biased, squares, norms = {}, {}, {}, {}
 
@@ -213,14 +208,15 @@ def tile_causalwaveletfieldattentionbyte_pa_kernel(tc, x, k_w, k_b, v_w, v_b, sc
             pr = u // 8
             sums[u] = bank(bk)
             for ti in range(2):
-                t = 2 * (u % 8) + ti
                 for gg in range(2):
+                    xc = (u % 8) * SLAB + gg * 256 + ti * P
+                    wc = pr * SLAB + gg * 256
                     nc.tensor.matmul_mx(
                         out=sums[u][:, ti * 256:(ti + 1) * 256],
-                        lhsT=xq_v[:, gg, t * P:(t + 1) * P].bitcast(FP8X4),
-                        lhsT_scale=xs_v[:, gg, t * P:(t + 1) * P],
-                        rhs=wq_v[:, gg, pr * 256:(pr + 1) * 256].bitcast(FP8X4),
-                        rhs_scale=ws_v[:, gg, pr * 256:(pr + 1) * 256],
+                        lhsT=xq[:, xc:xc + P].bitcast(FP8X4),
+                        lhsT_scale=xs[:, xc:xc + P],
+                        rhs=wq[:, wc:wc + 256].bitcast(FP8X4),
+                        rhs_scale=ws[:, wc:wc + 256],
                         start=(gg == 0),
                         stop=(gg == 1),
                     )

@@ -29,6 +29,7 @@ GROUP = 4 * ROW
 PAD = 8
 SHIFTS = ((2, 0, 1), (3, 1, 0), (6, 1, 1))
 QUICK = 12
+LESS = (13,)
 TAPS_LATER = ((), (), ((0, 0),), ((1, 2), (0, 1)), ((1, 1),), ((0, 2),), ((1, 0),), ())
 TAPS_SOON = ((), ((0, 0),), ((1, 2), (0, 1)), ((1, 1),), ((0, 2), (1, 0)), (), (), ())
 
@@ -93,7 +94,7 @@ def tile_causalwaveletfieldattentionbyte_pa_kernel(tc, x, k_w, k_b, v_w, v_b, sc
         def spread_biases(q, bk):
             bias_banks[q] = bank_bf(bk)
             for m in range(4 if q else 6):
-                source = 4 * q + m if m < 4 else 2 * PAIRS + m - 4
+                source = PAIRS * q + m if m < 4 else 2 * PAIRS + m - 4
                 column = small_columns[:, source:source + 1].to_broadcast([P, P])
                 nc.tensor.transpose(bias_banks[q][:, m * P:(m + 1) * P], column, ident_bf[:])
 
@@ -114,7 +115,9 @@ def tile_causalwaveletfieldattentionbyte_pa_kernel(tc, x, k_w, k_b, v_w, v_b, sc
             )
 
         def place(col, table, j):
-            return lambda: nc.vector.tensor_copy(out=rows[:, :, col:col + 1], in_=table[:, j, :].unsqueeze(2))
+            count = min(2, NS - j) if table is pow2 else min(2, NS - 1 - j)
+            out_cols = rows[:, :, col:count * col + 1:col]
+            return lambda: nc.vector.tensor_copy(out=out_cols, in_=table[:, j:j + count, :].rearrange("p j h -> p h j"))
 
         gain_steps = [
             lambda: nc.vector.tensor_reduce(out=gsum[:], in_=by_head, axis=AX.X, op=ALU.add),
@@ -126,8 +129,8 @@ def tile_causalwaveletfieldattentionbyte_pa_kernel(tc, x, k_w, k_b, v_w, v_b, sc
             add_t1,
             lambda: nc.vector.tensor_scalar_mul(out=rows[:, :, 0:1], in0=gone[:].unsqueeze(2), scalar1=T3),
         ]
-        gain_steps += [place(2 ** (j - 2), pow2, j) for j in range(2, NS)]
-        gain_steps += [place(3 * 2 ** (j - 2), thr2, j) for j in range(2, NS - 1)]
+        gain_steps += [place(2 ** (j - 2), pow2, j) for j in range(2, NS, 2)]
+        gain_steps += [place(3 * 2 ** (j - 2), thr2, j) for j in range(2, NS - 1, 2)]
 
         def take_gain_steps(count):
             for step in gain_steps[0:count]:
@@ -202,7 +205,7 @@ def tile_causalwaveletfieldattentionbyte_pa_kernel(tc, x, k_w, k_b, v_w, v_b, sc
                 in_=grouped[slab][:],
             )
 
-        sums, biased, squares, norms = {}, {}, {}, {}
+        sums, biased, step_total, norms = {}, {}, {}, {}
 
         def project(u, bk):
             pr = u // 8
@@ -232,25 +235,30 @@ def tile_causalwaveletfieldattentionbyte_pa_kernel(tc, x, k_w, k_b, v_w, v_b, sc
                 op=ALU.add,
             )
 
-        def square(u):
-            squares[u] = small.tile([P, 4], F32, tag="msq", name="msq")
-            for th in range(4):
-                lo = (th // 2) * 256 + (th % 2) * HD
-                nc.scalar.activation(
-                    out=biased[u][:, lo:lo + HD], in_=biased[u][:, lo:lo + HD], func=ACT.Square,
-                    accum_out=squares[u][:, th:th + 1],
-                )
+        def square(units):
+            total = small.tile([P, 8], F32, tag="msq", name="msq")
+            for n, u in enumerate(units):
+                for th in range(4):
+                    lo = (th // 2) * 256 + (th % 2) * HD
+                    nc.scalar.activation(
+                        out=biased[u][:, lo:lo + HD], in_=biased[u][:, lo:lo + HD], func=ACT.Square,
+                        accum_out=total[:, 4 * n + th:4 * n + th + 1],
+                    )
+            step_total[units[0]] = total
 
-        def root(u):
-            norms[u] = small.tile([P, 4], F32, tag="mag", name="mag")
-            nc.scalar.activation(out=norms[u][:], in_=squares[u][:], func=ACT.Sqrt)
+        def root(units):
+            norm = small.tile([P, 8], F32, tag="mag", name="mag")
+            width = 4 * len(units)
+            nc.scalar.activation(out=norm[:, 0:width], in_=step_total[units[0]][:, 0:width], func=ACT.Sqrt)
+            for n, u in enumerate(units):
+                norms[u] = norm[:, 4 * n:4 * n + 4]
 
         def make_field(u):
             pr, t = u // 8, 2 * (u % 8)
             nc.gpsimd.tensor_tensor(
                 out=field_v[:, t % 8:t % 8 + 2, 2 * pr:2 * pr + 2, t // 8, :],
                 in0=biased[u][:].rearrange("p (t m h c) -> p t m h c", t=2, m=2, h=2)[:, :, 1, :, :],
-                in1=norms[u][:].rearrange("p (t h) -> p t h", t=2).unsqueeze(3).to_broadcast([P, 2, 2, HD]),
+                in1=norms[u].rearrange("p (t h) -> p t h", t=2).unsqueeze(3).to_broadcast([P, 2, 2, HD]),
                 op=ALU.mult,
             )
 
@@ -263,7 +271,7 @@ def tile_causalwaveletfieldattentionbyte_pa_kernel(tc, x, k_w, k_b, v_w, v_b, sc
         def stationary(h, q):
             return field_v[:, q, h, :, :].rearrange("p b c -> p (b c)")
 
-        copy_f, toeplitz, result, taps = {}, {}, {}, {}
+        copy_f, toeplitz, result, taps, second_tap = {}, {}, {}, {}, {}
 
         def open_head(h):
             for half in range(2):
@@ -299,6 +307,12 @@ def tile_causalwaveletfieldattentionbyte_pa_kernel(tc, x, k_w, k_b, v_w, v_b, sc
                 scale=pow2[:, 0, h:h + 1],
             )
 
+        def shift_two(h):
+            second_tap[h] = accp.tile([P, HALF], F32, tag="second", name="second", bufs=1)
+            nc.scalar.activation(
+                out=in_order(second_tap[h][:]), in_=planes(copy_f[h, 1][:]), func=ACT.Copy, scale=pow2[:, 1, h:h + 1]
+            )
+
         def tap(h, half, which):
             shift, table, j = SHIFTS[which]
             window = in_order(taps[h][:, half * HALF + shift:half * HALF + shift + HALF])
@@ -318,6 +332,9 @@ def tile_causalwaveletfieldattentionbyte_pa_kernel(tc, x, k_w, k_b, v_w, v_b, sc
             lo = 1 - half
             res = result[h, half][:, lo:HALF]
             nc.gpsimd.tensor_tensor(out=res, in0=res, in1=taps[h][:, half * HALF + lo:(half + 1) * HALF], op=ALU.add)
+            if half == 1 and h in second_tap:
+                res = result[h, 1][:, 2:HALF]
+                nc.gpsimd.tensor_tensor(out=res, in0=res, in1=second_tap[h][:, 0:HALF - 2], op=ALU.add)
             store(h, half)
 
         def finish_on_vector(h, half):
@@ -334,12 +351,16 @@ def tile_causalwaveletfieldattentionbyte_pa_kernel(tc, x, k_w, k_b, v_w, v_b, sc
         made = []
 
         def later_stages(s):
-            for back, stage in ((1, add_bias), (2, square), (3, root), (3, make_field)):
-                if 0 <= s - back < len(made):
-                    for u in made[s - back]:
-                        stage(u)
-                        if back == 1:
-                            take_gain_steps(2)
+            units = {back: made[s - back] if 0 <= s - back < len(made) else [] for back in (1, 2, 3)}
+            for u in units[1]:
+                add_bias(u)
+                take_gain_steps(2)
+            if units[2]:
+                square(units[2])
+            if units[3]:
+                root(units[3])
+            for u in units[3]:
+                make_field(u)
 
         load_slab(slabs[0])
         load_slab(slabs[1])
@@ -363,22 +384,21 @@ def tile_causalwaveletfieldattentionbyte_pa_kernel(tc, x, k_w, k_b, v_w, v_b, sc
                     made[s].append(u)
             if s == 1:
                 turn_biases(2)
-            if s in (2, 3):
-                spread_biases(2 * s - 4, a + 2)
-                spread_biases(2 * s - 3, a + 3)
+            if s == 2:
+                spread_biases(0, 2)
+                spread_biases(1, 3)
             if s == 1:
                 nc.vector.tensor_copy(out=small_columns[:], in_=bias_banks["columns"][:, 0:P])
             if s >= 1:
                 regroup(slabs[s - 1], 0)
                 regroup(slabs[s - 1], 1)
-            if s in (3, 4):
-                for q in (2 * s - 6, 2 * s - 5):
-                    nc.vector.tensor_copy(out=biases[:, q * 512:(q + 1) * 512], in_=bias_banks[q][:, 0:512])
+            if s == 3:
+                for q in range(2):
+                    nc.vector.tensor_copy(out=biases[:, q * C:q * C + 512], in_=bias_banks[q][:, 0:512])
+                gains_top()
             later_stages(s)
             if s >= 1:
                 quantise(slabs[s - 1])
-            if s == 3:
-                gains_top()
             if s == 4:
                 nc.scalar.activation(out=g[:], in_=g[:], func=ACT.Exp)
             if s == 5:
@@ -390,6 +410,8 @@ def tile_causalwaveletfieldattentionbyte_pa_kernel(tc, x, k_w, k_b, v_w, v_b, sc
                 rows_out(nc.sync, 1, 4)
                 for gi in range(4):
                     blocks_back(nc.sync, gi)
+                nc.sync.dma_start(out=biases[:, 512:C], in_=k_b[512:C].partition_broadcast(P))
+                nc.sync.dma_start(out=biases[:, C + 512:2 * C], in_=v_b[512:C].partition_broadcast(P))
 
         for k, banks in enumerate(((0, 1), (6, 4), (7, 5), (3, 2))):
             s = early + k
@@ -431,11 +453,14 @@ def tile_causalwaveletfieldattentionbyte_pa_kernel(tc, x, k_w, k_b, v_w, v_b, sc
                     open_head(hh)
                 if age < 2:
                     shift_one(hh, age)
+                if age == 1 and hh in LESS:
+                    shift_two(hh)
             later_stages(first_slot + i)
             for hh, age in active:
                 schedule = TAPS_LATER if hh < QUICK else TAPS_SOON
                 for half, which in schedule[age]:
-                    tap(hh, half, which)
+                    if hh not in LESS or (half, which) != (1, 0):
+                        tap(hh, half, which)
                 if i == (4 * hh + 6 if hh < QUICK else 4 * hh + 4):
                     finish(hh, 0)
                 if hh == H - 1 and i == 4 * H:

from contextlib import ExitStack

import concourse.mybir as mybir
from concourse.masks import make_identity

F32 = mybir.dt.float32
BF16 = mybir.dt.bfloat16
U32 = mybir.dt.uint32
U8 = mybir.dt.uint8
FP8X4 = mybir.dt.float8_e4m3fn_x4
ALU = mybir.AluOpType
ACT = mybir.ActivationFunctionType
AX = mybir.AxisListType

P = 128
B, N, D, C, H, NS = 2, 1024, 1024, 1024, 16, 10
HD = C // H
HALF = N // 2
T0, T1, T2, T3 = (0.4829629131445341, 0.8365163037378079, 0.2241438680420134, -0.1294095225512604)

PAIRS = H // 2
UNITS = 8 * PAIRS
XSLABS = 8
AHEAD = 24
EARLY_PAIRS = 4
RAW_BUFS = 9
ROW = 320
GROUP = 4 * ROW
PAD = 8
SHIFTS = ((2, 0, 1), (3, 1, 0), (6, 1, 1))
QUICK = 12
LESS = (13,)
TAPS_LATER = ((), (), ((0, 0),), ((1, 2), (0, 1)), ((1, 1),), ((0, 2),), ((1, 0),), ())
TAPS_SOON = ((), ((0, 0),), ((1, 2), (0, 1)), ((1, 1),), ((0, 2), (1, 0)), (), (), ())

FLOPS = 2 * (B * N) * D * (2 * C)


def tile_causalwaveletfieldattentionbyte_pa_kernel(tc, x, k_w, k_b, v_w, v_b, scale_gain, out):
    nc = tc.nc
    with ExitStack() as ctx:
        const = ctx.enter_context(tc.tile_pool(name="const", bufs=1))
        rawp = ctx.enter_context(tc.tile_pool(name="rawp", bufs=RAW_BUFS))
        grpp = ctx.enter_context(tc.tile_pool(name="grpp", bufs=4))
        sortp = ctx.enter_context(tc.tile_pool(name="sortp", bufs=2))
        work = ctx.enter_context(tc.tile_pool(name="work", bufs=8))
        small = ctx.enter_context(tc.tile_pool(name="small", bufs=8))
        accp = ctx.enter_context(tc.tile_pool(name="accp", bufs=3))
        psum = ctx.enter_context(tc.psum_pool(name="psum", bufs=1))
        ctx.enter_context(tc.manual_schedule())

        def bank(i):
            return psum.tile([P, 512], F32, tag="b%d" % i, name="bank%d" % i)

        ident = const.tile([P, P], F32)
        make_identity(nc, ident[:])
        ident_bf = const.tile([P, P], BF16)
        make_identity(nc, ident_bf[:])

        biases = const.tile([P, 2 * C], BF16)
        small_rows = const.tile([P, P], BF16)
        small_columns = const.tile([P, P], BF16)
        nc.vector.memset(small_rows[:], 0.0)
        nc.scalar.dma_start(out=small_rows[0:PAIRS, :], in_=k_b.rearrange("(m c) -> m c", c=P))
        nc.scalar.dma_start(out=small_rows[PAIRS:2 * PAIRS, :], in_=v_b.rearrange("(m c) -> m c", c=P))
        gain_logits = scale_gain.rearrange("j h -> (j h)")
        for m in range(2):
            part = gain_logits[m * P:min(NS * H, (m + 1) * P)].rearrange("(o c) -> o c", o=1)
            nc.scalar.dma_start(out=small_rows[2 * PAIRS + m:2 * PAIRS + m + 1, 0:part.shape[1]], in_=part)

        g = const.tile([P, NS, H], F32)
        gmax = const.tile([P, H], F32)
        gsum = const.tile([P, H], F32)
        grec = const.tile([P, H], F32)
        gone = const.tile([P, H], F32)
        warm = const.tile([P, 1], F32)
        pow2 = const.tile([P, NS, H], F32)
        thr2 = const.tile([P, NS, H], F32)
        tables = (pow2, thr2)
        toep = const.tile([P, H * ROW], F32)
        scratch = out[1].rearrange("c n -> (c n)")
        by_head = g[:].rearrange("p j h -> p h j")

        nc.gpsimd.memset(toep[:], 0.0)
        bias_banks = {}

        def bank_bf(i):
            return psum.tile([P, 1024], BF16, tag="b%d" % i, name="bank_bf%d" % i)

        def turn_biases(bk):
            bias_banks["columns"] = bank_bf(bk)
            nc.tensor.transpose(bias_banks["columns"][:, 0:P], small_rows[:], ident_bf[:])

        def spread_biases(q, bk):
            bias_banks[q] = bank_bf(bk)
            for m in range(4 if q else 6):
                source = PAIRS * q + m if m < 4 else 2 * PAIRS + m - 4
                column = small_columns[:, source:source + 1].to_broadcast([P, P])
                nc.tensor.transpose(bias_banks[q][:, m * P:(m + 1) * P], column, ident_bf[:])

        def gains_top():
            logits = bias_banks[0][:, 512:512 + NS * H]
            nc.vector.tensor_copy(out=g[:], in_=logits.rearrange("p (j h) -> p j h", j=NS))
            nc.vector.tensor_reduce(out=gmax[:], in_=by_head, axis=AX.X, op=ALU.max)
            nc.vector.tensor_tensor(out=g[:], in0=g[:], in1=gmax[:].unsqueeze(1).to_broadcast([P, NS, H]), op=ALU.subtract)

        rows = toep[:].rearrange("p (h w) -> p h w", w=ROW)

        def divide():
            nc.vector.tensor_tensor(out=g[:], in0=g[:], in1=grec[:].unsqueeze(1).to_broadcast([P, NS, H]), op=ALU.mult)

        def add_t1():
            nc.vector.scalar_tensor_tensor(
                out=pow2[:, 1:NS, :], in0=g[:, 0:NS - 1, :], scalar=T1, in1=pow2[:, 1:NS, :], op0=ALU.mult, op1=ALU.add
            )

        def place(col, table, j):
            count = min(2, NS - j) if table is pow2 else min(2, NS - 1 - j)
            out_cols = rows[:, :, col:count * col + 1:col]
            return lambda: nc.vector.tensor_copy(out=out_cols, in_=table[:, j:j + count, :].rearrange("p j h -> p h j"))

        gain_steps = [
            lambda: nc.vector.tensor_reduce(out=gsum[:], in_=by_head, axis=AX.X, op=ALU.add),
            lambda: nc.vector.reciprocal(out=grec[:], in_=gsum[:]),
            divide,
            lambda: nc.vector.tensor_scalar_mul(out=pow2[:], in0=g[:], scalar1=T2),
            lambda: nc.vector.tensor_scalar_mul(out=thr2[:], in0=g[:], scalar1=T0),
            lambda: nc.vector.tensor_reduce(out=gone[:], in_=by_head, axis=AX.X, op=ALU.add),
            add_t1,
            lambda: nc.vector.tensor_scalar_mul(out=rows[:, :, 0:1], in0=gone[:].unsqueeze(2), scalar1=T3),
        ]
        gain_steps += [place(2 ** (j - 2), pow2, j) for j in range(2, NS, 2)]
        gain_steps += [place(3 * 2 ** (j - 2), thr2, j) for j in range(2, NS - 1, 2)]

        def take_gain_steps(count):
            for step in gain_steps[0:count]:
                step()
                gain_steps.remove(step)

        def rows_out(queue, g0, g1):
            queue.dma_start(
                out=scratch[g0 * P * GROUP:g1 * P * GROUP].rearrange("(g a w) -> a g w", a=P, w=GROUP),
                in_=toep[:, g0 * GROUP:g1 * GROUP].rearrange("p (g w) -> p g w", w=GROUP),
            )

        def blocks_back(queue, gi):
            used = 3 * ROW + 2 * P
            skewed = scratch[gi * P * GROUP:gi * P * GROUP + P * (GROUP - 1)].rearrange("(a w) -> a w", w=GROUP - 1)
            queue.dma_start(out=toep[:, gi * GROUP:gi * GROUP + used], in_=skewed[:, 0:used])

        xq = const.tile([P, 2 * B * N], U32, align_bytes=256)
        xs = const.tile([P, 2 * B * N], U8, align_bytes=256)
        wq = const.tile([P, 2 * 2 * C], U32, align_bytes=256)
        ws = const.tile([P, 2 * 2 * C], U8, align_bytes=256)
        SLAB = 512

        field = const.tile([P, 8 * H * 2 * HD], F32)
        field_v = field[:].rearrange("p (q h b c) -> p q h b c", q=8, h=H, b=2)

        raw, sorted_words, flipped, grouped = {}, {}, {}, {}

        def load_slab(slab):
            kind, i = slab
            raw[slab] = rawp.tile([P, 2 * D], BF16, tag="raw", name="raw")
            halves = raw[slab][:].rearrange("p (r d) -> p r d", r=2)
            if kind == "x":
                tokens = x[i // 4, ((i // 2) % 2) * HALF:((i // 2) % 2 + 1) * HALF, :].rearrange("(a r) d -> a r d", r=4)
                nc.sync.dma_start(out=halves, in_=tokens[:, 2 * (i % 2):2 * (i % 2) + 2, :])
            else:
                for lo in range(0, D, D // 2 if i == 0 else D):
                    hi = lo + (D // 2 if i == 0 else D)
                    nc.sync.dma_start(out=halves[:, 0, lo:hi], in_=k_w[i * P:(i + 1) * P, lo:hi])
                nc.sync.dma_start(out=halves[:, 1, :], in_=v_w[i * P:(i + 1) * P, :])

        def sort_words(slab, j):
            sorted_words[slab, j] = sortp.tile([P, D], BF16, tag="sorted", name="sorted")
            nc.scalar.copy(
                out=sorted_words[slab, j][:].bitcast(F32).rearrange("p (q u w) -> p q u w", u=2, w=P),
                in_=raw[slab][:, j * D:(j + 1) * D].bitcast(F32).rearrange("p (q w u) -> p q u w", u=2, w=P),
            )

        def flip(slab, j, bk):
            flipped[slab, j] = bank(bk)
            for gg in range(2):
                for u in range(2):
                    if (slab, j) in sorted_words:
                        lo = gg * 256 + u * P
                        words = sorted_words[slab, j][:].bitcast(F32)[:, lo:lo + P]
                    else:
                        lo = j * 512 + gg * 256
                        words = raw[slab][:].bitcast(F32)[:, lo + u:lo + 256:2]
                    nc.tensor.transpose(flipped[slab, j][:, (2 * gg + u) * P:(2 * gg + u + 1) * P], words, ident[:])

        def regroup(slab, j):
            if j == 0:
                grouped[slab] = grpp.tile([P, 2 * C], BF16, tag="grp", align_bytes=64, name="grp")
            dst = grouped[slab][:].bitcast(F32).rearrange("p (g c u) -> p g c u", g=2, u=2)[:, :, j * P:(j + 1) * P, :]
            nc.scalar.copy(out=dst, in_=flipped[slab, j][:].rearrange("p (g u c) -> p g c u", g=2, u=2))

        def quantise(slab):
            kind, i = slab
            codes, scales = (xq, xs) if kind == "x" else (wq, ws)
            nc.vector.quantize_mx(
                out=codes[:, i * SLAB:(i + 1) * SLAB].bitcast(FP8X4), scales=scales[:, i * SLAB:(i + 1) * SLAB],
                in_=grouped[slab][:],
            )

        sums, biased, step_total, norms = {}, {}, {}, {}

        def project(u, bk):
            pr = u // 8
            sums[u] = bank(bk)
            for ti in range(2):
                for gg in range(2):
                    xc = (u % 8) * SLAB + gg * 256 + ti * P
                    wc = pr * SLAB + gg * 256
                    nc.tensor.matmul_mx(
                        out=sums[u][:, ti * 256:(ti + 1) * 256],
                        lhsT=xq[:, xc:xc + P].bitcast(FP8X4),
                        lhsT_scale=xs[:, xc:xc + P],
                        rhs=wq[:, wc:wc + 256].bitcast(FP8X4),
                        rhs_scale=ws[:, wc:wc + 256],
                        start=(gg == 0),
                        stop=(gg == 1),
                    )

        def add_bias(u):
            pr = u // 8
            biased[u] = work.tile([P, 512], F32, tag="kv", name="kv")
            pair = biases[:].rearrange("p (m c) -> p m c", m=2)[:, :, pr * P:(pr + 1) * P]
            nc.vector.tensor_tensor(
                out=biased[u][:].rearrange("p (t m c) -> p t m c", t=2, m=2),
                in0=sums[u][:].rearrange("p (t m c) -> p t m c", t=2, m=2),
                in1=pair.unsqueeze(1).to_broadcast([P, 2, 2, P]),
                op=ALU.add,
            )

        def square(units):
            total = small.tile([P, 8], F32, tag="msq", name="msq")
            for n, u in enumerate(units):
                for th in range(4):
                    lo = (th // 2) * 256 + (th % 2) * HD
                    nc.scalar.activation(
                        out=biased[u][:, lo:lo + HD], in_=biased[u][:, lo:lo + HD], func=ACT.Square,
                        accum_out=total[:, 4 * n + th:4 * n + th + 1],
                    )
            step_total[units[0]] = total

        def root(units):
            norm = small.tile([P, 8], F32, tag="mag", name="mag")
            width = 4 * len(units)
            nc.scalar.activation(out=norm[:, 0:width], in_=step_total[units[0]][:, 0:width], func=ACT.Sqrt)
            for n, u in enumerate(units):
                norms[u] = norm[:, 4 * n:4 * n + 4]

        def make_field(u):
            pr, t = u // 8, 2 * (u % 8)
            nc.gpsimd.tensor_tensor(
                out=field_v[:, t % 8:t % 8 + 2, 2 * pr:2 * pr + 2, t // 8, :],
                in0=biased[u][:].rearrange("p (t m h c) -> p t m h c", t=2, m=2, h=2)[:, :, 1, :, :],
                in1=norms[u].rearrange("p (t h) -> p t h", t=2).unsqueeze(3).to_broadcast([P, 2, 2, HD]),
                op=ALU.mult,
            )

        def in_order(ap):
            return ap.rearrange("p (a r) -> p a r", r=4)

        def planes(ap):
            return ap.rearrange("p (r a) -> p a r", r=4)

        def stationary(h, q):
            return field_v[:, q, h, :, :].rearrange("p b c -> p (b c)")

        copy_f, toeplitz, result, taps, second_tap = {}, {}, {}, {}, {}

        def open_head(h):
            for half in range(2):
                copy_f[h, half] = bank(2 * (h % 2) + half)
                for r in range(4):
                    nc.tensor.transpose(copy_f[h, half][:, r * P:(r + 1) * P], stationary(h, 4 * half + r), ident[:])
            taps[h] = accp.tile([P, N + PAD], F32, tag="taps", name="taps")
            nc.gpsimd.memset(taps[h][:, N + 1:N + PAD], 0.0)

        def filter_matmul(h, i):
            near = toep[:, h * ROW:h * ROW + P]
            far = toep[:, h * ROW + P:h * ROW + 2 * P]
            if i == 0 or i == 4:
                toeplitz[h, i // 4] = bank(4 + i // 4)
            if i < 4:
                nc.tensor.matmul(toeplitz[h, 0][:, i * P:(i + 1) * P], lhsT=stationary(h, i), rhs=near, start=True, stop=True)
            else:
                r = (i - 4) // 2
                dst = toeplitz[h, 1][:, r * P:(r + 1) * P]
                if i % 2 == 0:
                    nc.tensor.matmul(dst, lhsT=stationary(h, r), rhs=far, start=True, stop=False)
                else:
                    nc.tensor.matmul(dst, lhsT=stationary(h, 4 + r), rhs=near, start=False, stop=True)

        def empty_toeplitz(h, half):
            result[h, half] = accp.tile([P, HALF], F32, tag="res%d" % half, name="res")
            nc.scalar.copy(out=in_order(result[h, half][:]), in_=planes(toeplitz[h, half][:]))

        def shift_one(h, half):
            lo = half * HALF + 1
            nc.scalar.activation(
                out=in_order(taps[h][:, lo:lo + HALF]), in_=planes(copy_f[h, half][:]), func=ACT.Copy,
                scale=pow2[:, 0, h:h + 1],
            )

        def shift_two(h):
            second_tap[h] = accp.tile([P, HALF], F32, tag="second", name="second", bufs=1)
            nc.scalar.activation(
                out=in_order(second_tap[h][:]), in_=planes(copy_f[h, 1][:]), func=ACT.Copy, scale=pow2[:, 1, h:h + 1]
            )

        def tap(h, half, which):
            shift, table, j = SHIFTS[which]
            window = in_order(taps[h][:, half * HALF + shift:half * HALF + shift + HALF])
            nc.vector.scalar_tensor_tensor(
                out=window, in0=planes(copy_f[h, half][:]), scalar=tables[table][:, j, h:h + 1], in1=window,
                op0=ALU.mult, op1=ALU.add,
            )

        def store(h, half):
            for b in range(2):
                nc.sync.dma_start(
                    out=out[b, h * HD:(h + 1) * HD, half * HALF:(half + 1) * HALF],
                    in_=result[h, half][b * HD:(b + 1) * HD, :],
                )

        def finish(h, half):
            lo = 1 - half
            res = result[h, half][:, lo:HALF]
            nc.gpsimd.tensor_tensor(out=res, in0=res, in1=taps[h][:, half * HALF + lo:(half + 1) * HALF], op=ALU.add)
            if half == 1 and h in second_tap:
                res = result[h, 1][:, 2:HALF]
                nc.gpsimd.tensor_tensor(out=res, in0=res, in1=second_tap[h][:, 0:HALF - 2], op=ALU.add)
            store(h, half)

        def finish_on_vector(h, half):
            result[h, half] = accp.tile([P, HALF], F32, tag="res%d" % half, name="res")
            nc.vector.tensor_tensor(
                out=in_order(result[h, half][:]), in0=planes(toeplitz[h, half][:]),
                in1=in_order(taps[h][:, half * HALF:(half + 1) * HALF]), op=ALU.add,
            )
            store(h, half)

        slabs = [("w", 0), ("w", 1)] + [("x", i) for i in range(XSLABS)] + [("w", pr) for pr in range(2, PAIRS)]
        late = [(("w", EARLY_PAIRS + k // 2), k % 2) for k in range(2 * (PAIRS - EARLY_PAIRS))]

        made = []

        def later_stages(s):
            units = {back: made[s - back] if 0 <= s - back < len(made) else [] for back in (1, 2, 3)}
            for u in units[1]:
                add_bias(u)
                take_gain_steps(2)
            if units[2]:
                square(units[2])
            if units[3]:
                root(units[3])
            for u in units[3]:
                make_field(u)

        load_slab(slabs[0])
        load_slab(slabs[1])
        load_slab(slabs[2])
        load_slab(slabs[3])
        for slab in slabs[4:RAW_BUFS]:
            load_slab(slab)

        early = 2 + XSLABS + EARLY_PAIRS - 2
        for s in range(early):
            a = 4 * (s % 2)
            flip(slabs[s], 0, a)
            flip(slabs[s], 1, a + 1)
            if 1 <= s and s - 1 + RAW_BUFS < len(slabs):
                load_slab(slabs[s - 1 + RAW_BUFS])
            made.append([])
            if s >= 4:
                for pr in range(2):
                    u = 8 * pr + s - 4
                    project(u, a + 2 + pr)
                    made[s].append(u)
            if s == 1:
                turn_biases(2)
            if s == 2:
                spread_biases(0, 2)
                spread_biases(1, 3)
            if s == 1:
                nc.vector.tensor_copy(out=small_columns[:], in_=bias_banks["columns"][:, 0:P])
            if s >= 1:
                regroup(slabs[s - 1], 0)
                regroup(slabs[s - 1], 1)
            if s == 3:
                for q in range(2):
                    nc.vector.tensor_copy(out=biases[:, q * C:q * C + 512], in_=bias_banks[q][:, 0:512])
                gains_top()
            later_stages(s)
            if s >= 1:
                quantise(slabs[s - 1])
            if s == 4:
                nc.scalar.activation(out=g[:], in_=g[:], func=ACT.Exp)
            if s == 5:
                nc.scalar.activation(out=warm[:], in_=ident[:, 0:1], func=ACT.Sqrt)
            if s > 4:
                take_gain_steps(1)
            if s == 9:
                rows_out(nc.sync, 0, 1)
                rows_out(nc.sync, 1, 4)
                for gi in range(4):
                    blocks_back(nc.sync, gi)
                nc.sync.dma_start(out=biases[:, 512:C], in_=k_b[512:C].partition_broadcast(P))
                nc.sync.dma_start(out=biases[:, C + 512:2 * C], in_=v_b[512:C].partition_broadcast(P))

        for k, banks in enumerate(((0, 1), (6, 4), (7, 5), (3, 2))):
            s = early + k
            if k == 0:
                flip(late[0][0], late[0][1], 2)
            made.append([16 + 2 * k, 17 + 2 * k])
            for u, bk in zip(made[s], banks):
                project(u, bk)
            if k == 0:
                regroup(slabs[early - 1], 0)
                regroup(slabs[early - 1], 1)
            if k == 1:
                regroup(late[0][0], late[0][1])
            later_stages(s)
            if k == 0:
                quantise(slabs[early - 1])

        first_slot = len(made)

        def base(h):
            return 4 * h - max(0, h - QUICK)

        def slot(i):
            h, p = divmod(i, 4)
            if p == 0 and 1 <= h < len(late):
                regroup(late[h][0], late[h][1])
            if p == 0 and 0 <= h - 1 < H - 1:
                empty_toeplitz(h - 1, 1)
            if p == 2 and h < H:
                empty_toeplitz(h, 0)
            made.append([])
            u = AHEAD + 4 * h + p - min(h, len(late) - 1)
            if u < UNITS and (p < 3 or h + 1 >= len(late)):
                project(u, 6 + p % 2)
                made[first_slot + i].append(u)
            active = [(hh, i - base(hh)) for hh in range(H) if 0 <= i - base(hh) < 8]
            for hh, age in active:
                if age == 0 and hh > QUICK:
                    open_head(hh)
                if age < 2:
                    shift_one(hh, age)
                if age == 1 and hh in LESS:
                    shift_two(hh)
            later_stages(first_slot + i)
            for hh, age in active:
                schedule = TAPS_LATER if hh < QUICK else TAPS_SOON
                for half, which in schedule[age]:
                    if hh not in LESS or (half, which) != (1, 0):
                        tap(hh, half, which)
                if i == (4 * hh + 6 if hh < QUICK else 4 * hh + 4):
                    finish(hh, 0)
                if hh == H - 1 and i == 4 * H:
                    finish_on_vector(hh, 1)
                if hh < H - 1 and i == (4 * hh + 7 if hh < QUICK else 4 * hh + 5):
                    finish(hh, 1)
            if p == 2 and h % 2 == 1 and h < len(late):
                quantise(late[h][0])
            if p == 1 and h + 1 < len(late):
                sort_words(late[h + 1][0], late[h + 1][1])

        for h in range(H):
            if h <= QUICK:
                open_head(h)
            for i in range(12):
                filter_matmul(h, i)
                if i % 3 == 1 and i < 10:
                    slot(4 * h + i // 3)
            if h + 1 < len(late):
                flip(late[h + 1][0], late[h + 1][1], 7)
            slot(4 * h + 3)
        slot(4 * H)
